import numpy as np
import ml_dtypes


def mxq(x, axis, fmt="e4m3"):
    dtype, down = {"e4m3": (ml_dtypes.float8_e4m3fn, 7), "e5m2": (ml_dtypes.float8_e5m2, 14)}[fmt]
    v = np.moveaxis(np.asarray(x, np.float32).astype(ml_dtypes.bfloat16).astype(np.float64), axis, -1)
    blocks = v.reshape(v.shape[:-1] + (-1, 32))
    amax = np.abs(blocks).max(-1, keepdims=True)
    byte = np.maximum(np.where(amax > 0, np.frexp(amax)[1] - 1 + 127, 0) - down, 1)
    scale = np.exp2(byte - 127.0)
    codes = (blocks / scale).astype(np.float32).astype(dtype).astype(np.float64)
    return np.moveaxis((codes * scale).reshape(v.shape), -1, axis)


WIDE = False


def mx_kscale(k):
    if not WIDE:
        return np.ones(k)
    levels = np.array([10, -10, 5, -5, 0])
    if k % 512:
        return np.exp2(np.random.permutation(np.resize(levels, k // 32))).repeat(32)
    a = np.empty((k // 512, 16))
    for p in range(k // 512):
        a[p, :8] = np.random.permutation(np.resize(levels, 8))
        for g in range(8):
            far = levels[np.abs(levels - a[p, g]) >= 10]
            a[p, g + 8] = far[np.random.randint(len(far))]
    return np.exp2(a.ravel()).repeat(32)


BF16 = ml_dtypes.bfloat16


def bf(x):
    return np.asarray(x, np.float32).astype(BF16)


def f64(x):
    return np.asarray(x).astype(np.float64)


B, D_IN, UNITS = 1024, 512, 512


def sigmoid(v):
    return 1.0 / (1.0 + np.exp(-v))


def draw0():
    s, t = mx_kscale(D_IN), mx_kscale(UNITS)
    sx, sh = 1.0 / np.sqrt(D_IN), 1.0 / np.sqrt(UNITS)
    return {"input_x": bf(np.random.standard_normal((B, D_IN)) * s),
            "input_h": bf(np.random.standard_normal((B, UNITS)) * t),
            "Wx_r": bf(np.random.standard_normal((D_IN, UNITS)) * sx / s[:, None]),
            "b_r": bf(np.random.standard_normal(UNITS) * 0.5),
            "Wh_r": bf(np.random.standard_normal((UNITS, UNITS)) * sh / t[:, None]),
            "Wx_h": bf(np.random.standard_normal((D_IN, UNITS)) * sx / s[:, None]),
            "b_h": bf(np.random.standard_normal(UNITS) * 0.5),
            "Wh_h": bf(np.random.standard_normal((UNITS, UNITS)) * sh / t[:, None])}


def core(input_x, input_h, Wx_r, b_r, Wh_r, Wx_h, b_h, Wh_h):
    xq = mxq(f64(input_x), 1, "e4m3")
    hq = mxq(f64(input_h), 1, "e4m3")
    r = sigmoid((xq @ mxq(f64(Wx_r), 0, "e4m3")) + f64(b_r) + (hq @ mxq(f64(Wh_r), 0, "e4m3")))
    return np.tanh((xq @ mxq(f64(Wx_h), 0, "e4m3")) + f64(b_h) + r * (hq @ mxq(f64(Wh_h), 0, "e4m3")))


def e4m3fn_bytes(y):
    return np.clip(np.asarray(y, np.float64), -448.0, 448.0).astype(np.float32).astype(ml_dtypes.float8_e4m3fn).view(np.uint8)


def e4m3fn_values(b):
    return np.asarray(b, np.uint8).view(ml_dtypes.float8_e4m3fn).astype(np.float64)


def setup_inputs():
    d = draw0()
    x0 = np.asarray(d['input_x']).astype(np.float64)
    s = (np.max(np.abs(x0), axis=(0,), keepdims=True) / 448.0).astype(np.float32)
    out = {}
    for k, v in d.items():
        if k == 'input_x':
            out['input_x_bytes'] = e4m3fn_bytes(x0 / s.astype(np.float64))
            out['input_x_scale'] = s
        else:
            out[k] = v
    return out


def reference(input_x_bytes, input_x_scale, input_h, Wx_r, b_r, Wh_r, Wx_h, b_h, Wh_h):
    return core(e4m3fn_values(input_x_bytes) * input_x_scale.astype(np.float64), input_h, Wx_r, b_r, Wh_r, Wx_h, b_h, Wh_h)

@@ -1,0 +1,273 @@
+from contextlib import ExitStack
+
+import concourse.masks as masks
+import concourse.mybir as mybir
+
+B, D_IN, UNITS = 1024, 512, 512
+FLOPS = 4 * 2 * B * D_IN * UNITS
+
+F32 = mybir.dt.float32
+BF16 = mybir.dt.bfloat16
+U32 = mybir.dt.uint32
+U8 = mybir.dt.uint8
+FP8 = mybir.dt.float8_e4m3fn
+FP8X4 = mybir.dt.float8_e4m3fn_x4
+ACT = mybir.ActivationFunctionType
+ALU = mybir.AluOpType
+
+P = 128
+NA = 8
+
+
+def tile_augru_pa_kernel(tc, input_x_bytes, input_x_scale, input_h, Wx_r, b_r, Wh_r, Wx_h, b_h, Wh_h, out):
+    nc = tc.nc
+    xb_v = input_x_bytes.rearrange("(p a) k -> p a k", a=NA)
+    h_v = input_h.rearrange("(p a) k -> p a k", a=NA)
+    out_v = out.rearrange("(p a) u -> p a u", a=NA)
+    weights = {"xr": Wx_r, "hr": Wh_r, "hh": Wh_h, "xh": Wx_h}
+
+    with ExitStack() as ctx:
+        keep = ctx.enter_context(tc.tile_pool(name="keep", bufs=1))
+        psum = ctx.enter_context(tc.psum_pool(name="psum", bufs=8))
+        ctx.enter_context(tc.manual_schedule())
+
+        ident = keep.tile([P, P], F32, name="ident")
+        brows = keep.tile([P, P], BF16, name="brows")
+        browsf = keep.tile([P, P], F32, name="browsf")
+        bias = keep.tile([P, 8], F32, name="bias")
+        warm = keep.tile([P, 1], F32, name="warm")
+        warm2 = keep.tile([P, 1], F32, name="warm2")
+        xbytes = keep.tile([P, NA, D_IN], U8, name="xbytes")
+        xscale = keep.tile([P, D_IN], F32, name="xscale")
+        s4 = keep.tile([P, 4], F32, name="s4")
+        xw = keep.tile([P, NA, D_IN], BF16, name="xw")
+        hraw = keep.tile([P, NA, D_IN], BF16, name="hraw")
+        wraw, wg, wc, wsc = {}, {}, {}, {}
+        for w in weights:
+            wraw[w] = keep.tile([P, 4, UNITS], BF16, name="wraw_" + w)
+            wg[w] = keep.tile([P, 4 * UNITS], BF16, name="wg_" + w, align_bytes=64)
+            wc[w] = keep.tile([P, UNITS], U32, name="wc_" + w, align_bytes=64)
+            wsc[w] = keep.tile([P, UNITS], U8, name="wsc_" + w, align_bytes=64)
+        ag, ac, asc = {}, {}, {}
+        for s in ("x", "h"):
+            for hf in (0, 1):
+                ag[s, hf] = keep.tile([P, 2048], BF16, name="ag_%s%d" % (s, hf), align_bytes=64)
+                ac[s, hf] = keep.tile([P, 512], U32, name="ac_%s%d" % (s, hf), align_bytes=64)
+                asc[s, hf] = keep.tile([P, 512], U8, name="asc_%s%d" % (s, hf), align_bytes=64)
+        r, t2, t3, o = {}, {}, {}, {}
+        for i in range(8):
+            r[i] = keep.tile([P, 512], F32, name="r_%d" % i)
+            t2[i] = keep.tile([P, 512], F32, name="t2_%d" % i)
+            t3[i] = keep.tile([P, 512], F32, name="t3_%d" % i)
+            o[i] = keep.tile([P, 512], F32, name="o_%d" % i)
+        banks = {}
+
+        def bank(name):
+            banks[name] = psum.tile([P, 512], F32, name=name, tag="bank")
+            return banks[name]
+
+        def ld_w(w, n0=0, n1=UNITS):
+            nc.sync.dma_start(out=wraw[w][:, :, n0:n1], in_=weights[w].rearrange("(p j) n -> p j n", j=4)[:, :, n0:n1])
+
+        def ld_x(a0, a1):
+            nc.sync.dma_start(out=xbytes[:, a0:a1, :], in_=xb_v[:, a0:a1, :])
+
+        def ld_h(a0, a1):
+            nc.sync.dma_start(out=hraw[:, a0:a1, :], in_=h_v[:, a0:a1, :])
+
+        def ld_sc():
+            nc.sync.dma_start(out=s4[:], in_=input_x_scale.rearrange("o (p c) -> p (o c)", c=4))
+
+        def spread_sc():
+            bk = bank("Tsc")
+            for c4 in range(4):
+                nc.tensor.transpose(bk[:, P * c4 : P * c4 + P], s4[:, c4 : c4 + 1].to_broadcast([P, P]), ident[:])
+            nc.scalar.copy(out=xscale[:].rearrange("p (i c) -> p i c", c=4), in_=bk[:].rearrange("p (c i) -> p i c", c=4))
+
+        def il(w, eng, n0=0, n1=UNITS):
+            dst = wg[w][:, 4 * n0 : 4 * n1].rearrange("p (c i j) -> p c j i", i=4, j=4)
+            src = wraw[w][:, :, n0:n1].rearrange("p j (c i) -> p c j i", i=4)
+            if eng == "V":
+                nc.vector.tensor_copy(out=dst, in_=src)
+            elif eng == "S":
+                nc.scalar.copy(out=dst, in_=src)
+            else:
+                nc.gpsimd.tensor_scalar(out=dst, in0=src, scalar1=1.0, scalar2=0.0, op0=ALU.mult, op1=ALU.add)
+
+        def qw(w):
+            nc.vector.quantize_mx(out=wc[w][:].bitcast(FP8X4), scales=wsc[w][:], in_=wg[w][:])
+
+        def widen(a):
+            nc.vector.tensor_tensor(out=xw[:, a, :], in0=xbytes[:, a, :].bitcast(FP8), in1=xscale[:], op=ALU.mult)
+
+        def turn(s, j):
+            src = xw if s == "x" else hraw
+            bv = bank("T%s%d" % (s, j))[:].rearrange("p (a u r) -> p a u r", a=2, u=2)
+            for al in (0, 1):
+                words = src[:, 2 * j + al, :].bitcast(F32)
+                for u in (0, 1):
+                    nc.tensor.transpose(bv[:, al, u, :], words[:, u:256:2], ident[:])
+
+        def cp(s, j, eng="S"):
+            hf, jl = divmod(j, 2)
+            bv = banks["T%s%d" % (s, j)][:].rearrange("p (a u r) -> p a r u", a=2, u=2)
+            dst = ag[s, hf][:, 1024 * jl : 1024 * jl + 1024].bitcast(F32).rearrange("p (a r u) -> p a r u", a=2, u=2)
+            if eng == "S":
+                nc.scalar.copy(out=dst, in_=bv)
+            else:
+                nc.vector.tensor_copy(out=dst, in_=bv)
+
+        def qa(s, hf):
+            nc.vector.quantize_mx(out=ac[s, hf][:].bitcast(FP8X4), scales=asc[s, hf][:], in_=ag[s, hf][:])
+
+        def mx(dst, w, s, i, start, stop):
+            hf, m = divmod(i, 4)
+            cols = slice(P * m, P * m + P)
+            nc.tensor.matmul_mx(
+                out=dst[:],
+                lhsT=wc[w][:, cols].bitcast(FP8X4),
+                lhsT_scale=wsc[w][:, cols],
+                rhs=ac[s, hf][:].bitcast(FP8X4),
+                rhs_scale=asc[s, hf][:],
+                start=start,
+                stop=stop,
+            )
+
+        def a1(i):
+            mx(bank("a%d" % i), "xr", "x", i, True, False)
+
+        def a2(i):
+            mx(banks["a%d" % i], "hr", "h", i, False, True)
+
+        def sg(i):
+            m = i % 4
+            nc.scalar.activation(out=r[i][:], in_=banks["a%d" % i][:], func=ACT.Sigmoid, bias=bias[:, m : m + 1], scale=1.0)
+
+        def b(i):
+            mx(bank("b%d" % i), "hh", "h", i, True, True)
+
+        def o1(i):
+            nc.vector.tensor_tensor(out=t2[i][:], in0=r[i][:], in1=banks["b%d" % i][:], op=ALU.mult)
+
+        def c(i):
+            mx(bank("c%d" % i), "xh", "x", i, True, True)
+
+        def o2(i):
+            m = i % 4
+            nc.vector.scalar_tensor_tensor(
+                out=t3[i][:], in0=t2[i][:], scalar=bias[:, 4 + m : 5 + m], in1=banks["c%d" % i][:], op0=ALU.add, op1=ALU.add
+            )
+
+        def tt(i):
+            bk = bank("tt%d" % i)
+            for al in range(4):
+                nc.tensor.transpose(bk[:, P * al : P * al + P], t3[i][:, P * al : P * al + P], ident[:])
+
+        def th(i):
+            nc.scalar.activation(out=o[i][:], in_=banks["tt%d" % i][:], func=ACT.Tanh)
+
+        def st(i):
+            hf, m = divmod(i, 4)
+            nc.sync.dma_start(
+                out=out_v[:, 4 * hf : 4 * hf + 4, P * m : P * m + P], in_=o[i][:].rearrange("p (a u) -> p a u", a=4)
+            )
+
+        masks.make_identity(nc, ident[:])
+        nc.vector.memset(warm[:], 0.0)
+        nc.vector.memset(brows[:], 0.0)
+        nc.scalar.activation(out=warm2[:], in_=warm[:], func=ACT.Sigmoid)
+        nc.scalar.dma_start(out=brows[0:4, :], in_=b_r.rearrange("(m p) -> m p", p=P))
+        nc.scalar.dma_start(out=brows[4:8, :], in_=b_h.rearrange("(m p) -> m p", p=P))
+
+        ld_sc()
+        ld_w("xr", 0, 256)
+        ld_x(0, 2)
+        ld_w("xr", 256, 512)
+        ld_x(2, 4)
+        ld_w("hr")
+        ld_h(0, 4)
+        ld_w("hh")
+        ld_x(4, 8)
+        ld_w("xh")
+        ld_h(4, 8)
+
+        spread_sc()
+        il("xr", "V", 0, 256)
+        widen(0)
+        widen(1)
+        il("xr", "S", 256, 512)
+        turn("x", 0)
+        nc.vector.tensor_copy(out=browsf[:], in_=brows[:])
+        nc.tensor.transpose(bank("bb")[:, 0:P], browsf[:], ident[:])
+        widen(2)
+        widen(3)
+        turn("x", 1)
+        il("hr", "S", 0, 256)
+        il("hr", "V", 256, 512)
+        nc.vector.tensor_copy(out=bias[:], in_=banks["bb"][:, 0:8])
+        cp("x", 0)
+        cp("x", 1)
+        turn("h", 0)
+        turn("h", 1)
+        qw("xr")
+        qa("x", 0)
+        for i in range(4):
+            a1(i)
+        cp("h", 0)
+        cp("h", 1)
+        qw("hr")
+        qa("h", 0)
+        for i in range(4):
+            a2(i)
+        il("hh", "S")
+        widen(4)
+        widen(5)
+        turn("x", 2)
+        widen(6)
+        qw("hh")
+        for i in range(4):
+            b(i)
+        il("xh", "V", 0, 256)
+        for i in range(4):
+            sg(i)
+        il("xh", "S", 256, 512)
+        o1(0)
+        widen(7)
+        turn("x", 3)
+        turn("h", 2)
+        turn("h", 3)
+        o1(1)
+        o1(2)
+        qw("xh")
+        for i in range(4):
+            c(i)
+        cp("x", 2)
+        cp("x", 3)
+        qa("x", 1)
+        o1(3)
+        cp("h", 2)
+        cp("h", 3)
+        qa("h", 1)
+        for i in range(4, 8):
+            a1(i)
+        for i in range(4, 8):
+            a2(i)
+        for i in range(4):
+            o2(i)
+        for i in range(4, 8):
+            sg(i)
+        for i in range(4, 8):
+            b(i)
+        for i in range(4):
+            tt(i)
+            th(i)
+            st(i)
+        for i in range(4, 8):
+            c(i)
+        for i in range(4, 8):
+            o1(i)
+        for i in range(4, 8):
+            o2(i)
+            tt(i)
+            th(i)
+            st(i)

@@ -176,8 +176,8 @@ def tile_augru_pa_kernel(tc, input_x_bytes, input_x_scale, input_h, Wx_r, b_r, W
         nc.vector.memset(warm[:], 0.0)
         nc.vector.memset(brows[:], 0.0)
         nc.scalar.activation(out=warm2[:], in_=warm[:], func=ACT.Sigmoid)
-        nc.scalar.dma_start(out=brows[0:4, :], in_=b_r.rearrange("(m p) -> m p", p=P))
-        nc.scalar.dma_start(out=brows[4:8, :], in_=b_h.rearrange("(m p) -> m p", p=P))
+        nc.gpsimd.dma_start(out=brows[0:4, :], in_=b_r.rearrange("(m p) -> m p", p=P))
+        nc.gpsimd.dma_start(out=brows[4:8, :], in_=b_h.rearrange("(m p) -> m p", p=P))
 
         ld_sc()
         ld_w("xr", 0, 256)
@@ -197,20 +197,20 @@ def tile_augru_pa_kernel(tc, input_x_bytes, input_x_scale, input_h, Wx_r, b_r, W
         widen(1)
         il("xr", "S", 256, 512)
         turn("x", 0)
-        nc.vector.tensor_copy(out=browsf[:], in_=brows[:])
-        nc.tensor.transpose(bank("bb")[:, 0:P], browsf[:], ident[:])
         widen(2)
         widen(3)
         turn("x", 1)
         il("hr", "S", 0, 256)
         il("hr", "V", 256, 512)
-        nc.vector.tensor_copy(out=bias[:], in_=banks["bb"][:, 0:8])
         cp("x", 0)
         cp("x", 1)
         turn("h", 0)
         turn("h", 1)
         qw("xr")
+        nc.vector.tensor_copy(out=browsf[:], in_=brows[:])
+        nc.tensor.transpose(bank("bb")[:, 0:P], browsf[:], ident[:])
         qa("x", 0)
+        nc.vector.tensor_copy(out=bias[:], in_=banks["bb"][:, 0:8])
         for i in range(4):
             a1(i)
         cp("h", 0)

@@ -222,11 +222,11 @@ def tile_augru_pa_kernel(tc, input_x_bytes, input_x_scale, input_h, Wx_r, b_r, W
         il("hh", "S")
         widen(4)
         widen(5)
-        turn("x", 2)
         widen(6)
         qw("hh")
         for i in range(4):
             b(i)
+        turn("x", 2)
         il("xh", "V", 0, 256)
         for i in range(4):
             sg(i)

@@ -237,8 +237,8 @@ def tile_augru_pa_kernel(tc, input_x_bytes, input_x_scale, input_h, Wx_r, b_r, W
         turn("h", 2)
         turn("h", 3)
         o1(1)
-        o1(2)
         qw("xh")
+        o1(2)
         for i in range(4):
             c(i)
         cp("x", 2)

@@ -139,6 +139,10 @@ def tile_augru_pa_kernel(tc, input_x_bytes, input_x_scale, input_h, Wx_r, b_r, W
         def a2(i):
             mx(banks["a%d" % i], "hr", "h", i, False, True)
 
+        def keep_warm():
+            for q in range(2):
+                nc.tensor.matmul(bank("warm%d" % q)[:], wg["xr"][:, 0:P], wg["xr"][:, 0:512], start=True, stop=True)
+
         def sg(i):
             m = i % 4
             nc.scalar.activation(out=r[i][:], in_=banks["a%d" % i][:], func=ACT.Sigmoid, bias=bias[:, m : m + 1], scale=1.0)
@@ -234,6 +238,7 @@ def tile_augru_pa_kernel(tc, input_x_bytes, input_x_scale, input_h, Wx_r, b_r, W
         o1(0)
         widen(7)
         turn("x", 3)
+        keep_warm()
         turn("h", 2)
         turn("h", 3)
         o1(1)

@@ -33,7 +33,7 @@ def tile_augru_pa_kernel(tc, input_x_bytes, input_x_scale, input_h, Wx_r, b_r, W
 
         ident = keep.tile([P, P], F32, name="ident")
         brows = keep.tile([P, P], BF16, name="brows")
-        browsf = keep.tile([P, P], F32, name="browsf")
+        eye8 = keep.tile([P, 8], BF16, name="eye8")
         bias = keep.tile([P, 8], F32, name="bias")
         warm = keep.tile([P, 1], F32, name="warm")
         warm2 = keep.tile([P, 1], F32, name="warm2")
@@ -139,10 +139,6 @@ def tile_augru_pa_kernel(tc, input_x_bytes, input_x_scale, input_h, Wx_r, b_r, W
         def a2(i):
             mx(banks["a%d" % i], "hr", "h", i, False, True)
 
-        def keep_warm():
-            for q in range(2):
-                nc.tensor.matmul(bank("warm%d" % q)[:], wg["xr"][:, 0:P], wg["xr"][:, 0:512], start=True, stop=True)
-
         def sg(i):
             m = i % 4
             nc.scalar.activation(out=r[i][:], in_=banks["a%d" % i][:], func=ACT.Sigmoid, bias=bias[:, m : m + 1], scale=1.0)
@@ -176,12 +172,24 @@ def tile_augru_pa_kernel(tc, input_x_bytes, input_x_scale, input_h, Wx_r, b_r, W
                 out=out_v[:, 4 * hf : 4 * hf + 4, P * m : P * m + P], in_=o[i][:].rearrange("p (a u) -> p a u", a=4)
             )
 
+        def bb():
+            nc.tensor.matmul(bank("bb")[:, 0:8], brows[:], eye8[:], start=True, stop=True)
+
+        def bbcp(eng):
+            if eng == "V":
+                nc.vector.tensor_copy(out=bias[:], in_=banks["bb"][:, 0:8])
+            else:
+                nc.scalar.copy(out=bias[:], in_=banks["bb"][:, 0:8])
+
+
+        def dm(n):
+            for q in range(n):
+                nc.tensor.matmul(bank("warm%d" % q)[:], wg["xr"][:, 0:P], wg["xr"][:, 0:512], start=True, stop=True)
         masks.make_identity(nc, ident[:])
         nc.vector.memset(warm[:], 0.0)
         nc.vector.memset(brows[:], 0.0)
+        nc.vector.tensor_copy(out=eye8[:], in_=ident[:, 0:8])
         nc.scalar.activation(out=warm2[:], in_=warm[:], func=ACT.Sigmoid)
-        nc.gpsimd.dma_start(out=brows[0:4, :], in_=b_r.rearrange("(m p) -> m p", p=P))
-        nc.gpsimd.dma_start(out=brows[4:8, :], in_=b_h.rearrange("(m p) -> m p", p=P))
 
         ld_sc()
         ld_w("xr", 0, 256)
@@ -194,6 +202,8 @@ def tile_augru_pa_kernel(tc, input_x_bytes, input_x_scale, input_h, Wx_r, b_r, W
         ld_x(4, 8)
         ld_w("xh")
         ld_h(4, 8)
+        nc.sync.dma_start(out=brows[0:4, :], in_=b_r.rearrange("(m p) -> m p", p=P))
+        nc.sync.dma_start(out=brows[4:8, :], in_=b_h.rearrange("(m p) -> m p", p=P))
 
         spread_sc()
         il("xr", "V", 0, 256)
@@ -211,12 +221,10 @@ def tile_augru_pa_kernel(tc, input_x_bytes, input_x_scale, input_h, Wx_r, b_r, W
         turn("h", 0)
         turn("h", 1)
         qw("xr")
-        nc.vector.tensor_copy(out=browsf[:], in_=brows[:])
-        nc.tensor.transpose(bank("bb")[:, 0:P], browsf[:], ident[:])
         qa("x", 0)
-        nc.vector.tensor_copy(out=bias[:], in_=banks["bb"][:, 0:8])
         for i in range(4):
             a1(i)
+        bb()
         cp("h", 0)
         cp("h", 1)
         qw("hr")
@@ -224,28 +232,35 @@ def tile_augru_pa_kernel(tc, input_x_bytes, input_x_scale, input_h, Wx_r, b_r, W
         for i in range(4):
             a2(i)
         il("hh", "S")
+        bbcp("S")
         widen(4)
         widen(5)
         widen(6)
         qw("hh")
-        for i in range(4):
-            b(i)
+        b(0)
+        b(1)
+        b(2)
+        b(3)
         turn("x", 2)
         il("xh", "V", 0, 256)
-        for i in range(4):
-            sg(i)
         il("xh", "S", 256, 512)
-        o1(0)
+        sg(0)
+        sg(1)
+        sg(2)
+        sg(3)
         widen(7)
         turn("x", 3)
-        keep_warm()
+        qw("xh")
+        o1(0)
+        o1(1)
+        dm(2)
         turn("h", 2)
         turn("h", 3)
-        o1(1)
-        qw("xh")
         o1(2)
-        for i in range(4):
-            c(i)
+        c(0)
+        c(1)
+        c(2)
+        c(3)
         cp("x", 2)
         cp("x", 3)
         qa("x", 1)
@@ -253,26 +268,59 @@ def tile_augru_pa_kernel(tc, input_x_bytes, input_x_scale, input_h, Wx_r, b_r, W
         cp("h", 2)
         cp("h", 3)
         qa("h", 1)
-        for i in range(4, 8):
-            a1(i)
-        for i in range(4, 8):
-            a2(i)
-        for i in range(4):
-            o2(i)
-        for i in range(4, 8):
-            sg(i)
-        for i in range(4, 8):
-            b(i)
-        for i in range(4):
-            tt(i)
-            th(i)
-            st(i)
-        for i in range(4, 8):
-            c(i)
-        for i in range(4, 8):
-            o1(i)
-        for i in range(4, 8):
-            o2(i)
-            tt(i)
-            th(i)
-            st(i)
+        a1(4)
+        a1(5)
+        a1(6)
+        a1(7)
+        a2(4)
+        a2(5)
+        a2(6)
+        a2(7)
+        o2(0)
+        o2(1)
+        o2(2)
+        o2(3)
+        sg(4)
+        sg(5)
+        sg(6)
+        sg(7)
+        b(4)
+        b(5)
+        b(6)
+        b(7)
+        tt(0)
+        th(0)
+        st(0)
+        tt(1)
+        th(1)
+        st(1)
+        tt(2)
+        th(2)
+        st(2)
+        tt(3)
+        th(3)
+        st(3)
+        c(4)
+        c(5)
+        c(6)
+        c(7)
+        o1(4)
+        o1(5)
+        o1(6)
+        o1(7)
+        o2(4)
+        tt(4)
+        th(4)
+        st(4)
+        o2(5)
+        tt(5)
+        th(5)
+        st(5)
+        o2(6)
+        tt(6)
+        th(6)
+        st(6)
+        o2(7)
+        tt(7)
+        th(7)
+        st(7)

@@ -194,6 +194,8 @@ def tile_augru_pa_kernel(tc, input_x_bytes, input_x_scale, input_h, Wx_r, b_r, W
         ld_sc()
         ld_w("xr", 0, 256)
         ld_x(0, 2)
+        nc.sync.dma_start(out=brows[0:4, :], in_=b_r.rearrange("(m p) -> m p", p=P))
+        nc.sync.dma_start(out=brows[4:8, :], in_=b_h.rearrange("(m p) -> m p", p=P))
         ld_w("xr", 256, 512)
         ld_x(2, 4)
         ld_w("hr")
@@ -202,8 +204,6 @@ def tile_augru_pa_kernel(tc, input_x_bytes, input_x_scale, input_h, Wx_r, b_r, W
         ld_x(4, 8)
         ld_w("xh")
         ld_h(4, 8)
-        nc.sync.dma_start(out=brows[0:4, :], in_=b_r.rearrange("(m p) -> m p", p=P))
-        nc.sync.dma_start(out=brows[4:8, :], in_=b_h.rearrange("(m p) -> m p", p=P))
 
         spread_sc()
         il("xr", "V", 0, 256)

@@ -243,19 +243,19 @@ def tile_augru_pa_kernel(tc, input_x_bytes, input_x_scale, input_h, Wx_r, b_r, W
         b(3)
         turn("x", 2)
         il("xh", "V", 0, 256)
-        il("xh", "S", 256, 512)
         sg(0)
         sg(1)
         sg(2)
         sg(3)
+        il("xh", "S", 256, 512)
+        o1(0)
         widen(7)
         turn("x", 3)
-        qw("xh")
-        o1(0)
-        o1(1)
         dm(2)
         turn("h", 2)
         turn("h", 3)
+        o1(1)
+        qw("xh")
         o1(2)
         c(0)
         c(1)

@@ -28,7 +28,7 @@ def tile_augru_pa_kernel(tc, input_x_bytes, input_x_scale, input_h, Wx_r, b_r, W
 
     with ExitStack() as ctx:
         keep = ctx.enter_context(tc.tile_pool(name="keep", bufs=1))
-        psum = ctx.enter_context(tc.psum_pool(name="psum", bufs=8))
+        psum = ctx.enter_context(tc.psum_pool(name="psum", bufs=1))
         ctx.enter_context(tc.manual_schedule())
 
         ident = keep.tile([P, P], F32, name="ident")
@@ -62,8 +62,24 @@ def tile_augru_pa_kernel(tc, input_x_bytes, input_x_scale, input_h, Wx_r, b_r, W
             o[i] = keep.tile([P, 512], F32, name="o_%d" % i)
         banks = {}
 
+        slots = {}
+        for k, names in enumerate(
+            (
+                "Tsc a2 Th3 a7 tt3 tt7",
+                "Tx0 a3 warm c1 b5 c5",
+                "Tx1 b0 Th2 a5 tt0 c7",
+                "Th0 b1 c0 b4 c4",
+                "Th1 b2 a4 b6 c6",
+                "bb b3 a6 tt1 tt4",
+                "a0 Tx2 c2 b7 tt6",
+                "a1 Tx3 c3 tt2 tt5",
+            )
+        ):
+            for n in names.split(" "):
+                slots[n] = k
+
         def bank(name):
-            banks[name] = psum.tile([P, 512], F32, name=name, tag="bank")
+            banks[name] = psum.tile([P, 512], F32, name=name, tag="bank%d" % slots[name])
             return banks[name]
 
         def ld_w(w, n0=0, n1=UNITS):
@@ -175,16 +191,14 @@ def tile_augru_pa_kernel(tc, input_x_bytes, input_x_scale, input_h, Wx_r, b_r, W
         def bb():
             nc.tensor.matmul(bank("bb")[:, 0:8], brows[:], eye8[:], start=True, stop=True)
 
-        def bbcp(eng):
-            if eng == "V":
-                nc.vector.tensor_copy(out=bias[:], in_=banks["bb"][:, 0:8])
-            else:
-                nc.scalar.copy(out=bias[:], in_=banks["bb"][:, 0:8])
+        def bbcp():
+            nc.scalar.copy(out=bias[:], in_=banks["bb"][:, 0:8])
 
 
-        def dm(n):
-            for q in range(n):
-                nc.tensor.matmul(bank("warm%d" % q)[:], wg["xr"][:, 0:P], wg["xr"][:, 0:512], start=True, stop=True)
+        def keep_warm():
+            bk = bank("warm")
+            for q in range(2):
+                nc.tensor.matmul(bk[:], wg["xr"][:, 0:P], wg["xr"][:, 0:512], start=True, stop=True)
         masks.make_identity(nc, ident[:])
         nc.vector.memset(warm[:], 0.0)
         nc.vector.memset(brows[:], 0.0)
@@ -194,11 +208,11 @@ def tile_augru_pa_kernel(tc, input_x_bytes, input_x_scale, input_h, Wx_r, b_r, W
         ld_sc()
         ld_w("xr", 0, 256)
         ld_x(0, 2)
-        nc.sync.dma_start(out=brows[0:4, :], in_=b_r.rearrange("(m p) -> m p", p=P))
-        nc.sync.dma_start(out=brows[4:8, :], in_=b_h.rearrange("(m p) -> m p", p=P))
         ld_w("xr", 256, 512)
         ld_x(2, 4)
         ld_w("hr")
+        nc.sync.dma_start(out=brows[0:4, :], in_=b_r.rearrange("(m p) -> m p", p=P))
+        nc.sync.dma_start(out=brows[4:8, :], in_=b_h.rearrange("(m p) -> m p", p=P))
         ld_h(0, 4)
         ld_w("hh")
         ld_x(4, 8)
@@ -232,7 +246,7 @@ def tile_augru_pa_kernel(tc, input_x_bytes, input_x_scale, input_h, Wx_r, b_r, W
         for i in range(4):
             a2(i)
         il("hh", "S")
-        bbcp("S")
+        bbcp()
         widen(4)
         widen(5)
         widen(6)
@@ -241,28 +255,28 @@ def tile_augru_pa_kernel(tc, input_x_bytes, input_x_scale, input_h, Wx_r, b_r, W
         b(1)
         b(2)
         b(3)
-        turn("x", 2)
         il("xh", "V", 0, 256)
         sg(0)
         sg(1)
         sg(2)
         sg(3)
+        turn("x", 2)
         il("xh", "S", 256, 512)
         o1(0)
         widen(7)
         turn("x", 3)
-        dm(2)
+        keep_warm()
         turn("h", 2)
         turn("h", 3)
         o1(1)
         qw("xh")
         o1(2)
+        cp("x", 2)
+        cp("x", 3)
         c(0)
         c(1)
         c(2)
         c(3)
-        cp("x", 2)
-        cp("x", 3)
         qa("x", 1)
         o1(3)
         cp("h", 2)
@@ -288,6 +302,10 @@ def tile_augru_pa_kernel(tc, input_x_bytes, input_x_scale, input_h, Wx_r, b_r, W
         b(5)
         b(6)
         b(7)
+        o1(4)
+        o1(5)
+        o1(6)
+        o1(7)
         tt(0)
         th(0)
         st(0)
@@ -304,10 +322,6 @@ def tile_augru_pa_kernel(tc, input_x_bytes, input_x_scale, input_h, Wx_r, b_r, W
         c(5)
         c(6)
         c(7)
-        o1(4)
-        o1(5)
-        o1(6)
-        o1(7)
         o2(4)
         tt(4)
         th(4)

@@ -31,35 +31,35 @@ def tile_augru_pa_kernel(tc, input_x_bytes, input_x_scale, input_h, Wx_r, b_r, W
         psum = ctx.enter_context(tc.psum_pool(name="psum", bufs=1))
         ctx.enter_context(tc.manual_schedule())
 
-        ident = keep.tile([P, P], F32, name="ident")
+        ident = keep.tile([P, P], F32, name="ident", align_bytes=256)
         brows = keep.tile([P, P], BF16, name="brows")
         eye8 = keep.tile([P, 8], BF16, name="eye8")
         bias = keep.tile([P, 8], F32, name="bias")
         warm = keep.tile([P, 1], F32, name="warm")
         warm2 = keep.tile([P, 1], F32, name="warm2")
-        xbytes = keep.tile([P, NA, D_IN], U8, name="xbytes")
-        xscale = keep.tile([P, D_IN], F32, name="xscale")
+        xbytes = keep.tile([P, NA, D_IN], U8, name="xbytes", align_bytes=256)
+        xscale = keep.tile([P, D_IN], F32, name="xscale", align_bytes=256)
         s4 = keep.tile([P, 4], F32, name="s4")
-        xw = keep.tile([P, NA, D_IN], BF16, name="xw")
-        hraw = keep.tile([P, NA, D_IN], BF16, name="hraw")
+        xw = keep.tile([P, NA, D_IN], BF16, name="xw", align_bytes=256)
+        hraw = keep.tile([P, NA, D_IN], BF16, name="hraw", align_bytes=256)
         wraw, wg, wc, wsc = {}, {}, {}, {}
         for w in weights:
-            wraw[w] = keep.tile([P, 4, UNITS], BF16, name="wraw_" + w)
-            wg[w] = keep.tile([P, 4 * UNITS], BF16, name="wg_" + w, align_bytes=64)
-            wc[w] = keep.tile([P, UNITS], U32, name="wc_" + w, align_bytes=64)
-            wsc[w] = keep.tile([P, UNITS], U8, name="wsc_" + w, align_bytes=64)
+            wraw[w] = keep.tile([P, 4, UNITS], BF16, name="wraw_" + w, align_bytes=256)
+            wg[w] = keep.tile([P, 4 * UNITS], BF16, name="wg_" + w, align_bytes=256)
+            wc[w] = keep.tile([P, UNITS], U32, name="wc_" + w, align_bytes=256)
+            wsc[w] = keep.tile([P, UNITS], U8, name="wsc_" + w, align_bytes=256)
         ag, ac, asc = {}, {}, {}
         for s in ("x", "h"):
             for hf in (0, 1):
-                ag[s, hf] = keep.tile([P, 2048], BF16, name="ag_%s%d" % (s, hf), align_bytes=64)
-                ac[s, hf] = keep.tile([P, 512], U32, name="ac_%s%d" % (s, hf), align_bytes=64)
-                asc[s, hf] = keep.tile([P, 512], U8, name="asc_%s%d" % (s, hf), align_bytes=64)
+                ag[s, hf] = keep.tile([P, 2048], BF16, name="ag_%s%d" % (s, hf), align_bytes=256)
+                ac[s, hf] = keep.tile([P, 512], U32, name="ac_%s%d" % (s, hf), align_bytes=256)
+                asc[s, hf] = keep.tile([P, 512], U8, name="asc_%s%d" % (s, hf), align_bytes=256)
         r, t2, t3, o = {}, {}, {}, {}
         for i in range(8):
-            r[i] = keep.tile([P, 512], F32, name="r_%d" % i)
-            t2[i] = keep.tile([P, 512], F32, name="t2_%d" % i)
-            t3[i] = keep.tile([P, 512], F32, name="t3_%d" % i)
-            o[i] = keep.tile([P, 512], F32, name="o_%d" % i)
+            r[i] = keep.tile([P, 512], F32, name="r_%d" % i, align_bytes=256)
+            t2[i] = keep.tile([P, 512], F32, name="t2_%d" % i, align_bytes=256)
+            t3[i] = keep.tile([P, 512], F32, name="t3_%d" % i, align_bytes=256)
+            o[i] = keep.tile([P, 512], F32, name="o_%d" % i, align_bytes=256)
         banks = {}
 
         slots = {}

@@ -65,14 +65,14 @@ def tile_augru_pa_kernel(tc, input_x_bytes, input_x_scale, input_h, Wx_r, b_r, W
         slots = {}
         for k, names in enumerate(
             (
-                "Tsc a2 Th3 a7 tt3 tt7",
-                "Tx0 a3 warm c1 b5 c5",
-                "Tx1 b0 Th2 a5 tt0 c7",
-                "Th0 b1 c0 b4 c4",
-                "Th1 b2 a4 b6 c6",
-                "bb b3 a6 tt1 tt4",
-                "a0 Tx2 c2 b7 tt6",
-                "a1 Tx3 c3 tt2 tt5",
+                "Tsc a2 a6 b6 tt4",
+                "Tx0 a3 a7 b7 tt5",
+                "Tx1 Tx2 b2 c2 tt2 tt6",
+                "Th0 Tx3 b3 c3 tt3 tt7",
+                "Th1 b0 c0 tt0 c6",
+                "bb b1 c1 tt1 c7",
+                "a0 Th2 a4 b4 c4",
+                "a1 Th3 a5 b5 c5",
             )
         ):
             for n in names.split(" "):
@@ -232,6 +232,7 @@ def tile_augru_pa_kernel(tc, input_x_bytes, input_x_scale, input_h, Wx_r, b_r, W
         il("hr", "V", 256, 512)
         cp("x", 0)
         cp("x", 1)
+        il("hh", "S", 0, 128)
         turn("h", 0)
         turn("h", 1)
         qw("xr")
@@ -242,54 +243,53 @@ def tile_augru_pa_kernel(tc, input_x_bytes, input_x_scale, input_h, Wx_r, b_r, W
         cp("h", 0)
         cp("h", 1)
         qw("hr")
+        widen(4)
         qa("h", 0)
         for i in range(4):
             a2(i)
-        il("hh", "S")
+        il("hh", "S", 128, 512)
         bbcp()
-        widen(4)
         widen(5)
         widen(6)
+        widen(7)
         qw("hh")
+        turn("x",2)
+        turn("x",3)
         b(0)
         b(1)
-        b(2)
-        b(3)
         il("xh", "V", 0, 256)
+        il("xh", "S", 256, 512)
+        qw("xh")
         sg(0)
         sg(1)
-        sg(2)
-        sg(3)
-        turn("x", 2)
-        il("xh", "S", 256, 512)
+        turn("h",2)
+        turn("h",3)
         o1(0)
-        widen(7)
-        turn("x", 3)
-        keep_warm()
-        turn("h", 2)
-        turn("h", 3)
         o1(1)
-        qw("xh")
-        o1(2)
-        cp("x", 2)
-        cp("x", 3)
+        cp("x",2)
+        cp("x",3)
+        cp("h",2)
+        cp("h",3)
         c(0)
         c(1)
-        c(2)
-        c(3)
-        qa("x", 1)
-        o1(3)
-        cp("h", 2)
-        cp("h", 3)
-        qa("h", 1)
+        b(2)
+        b(3)
+        qa("x",1)
         a1(4)
         a1(5)
-        a1(6)
-        a1(7)
+        qa("h",1)
+        sg(2)
+        sg(3)
         a2(4)
         a2(5)
+        a1(6)
         a2(6)
+        a1(7)
         a2(7)
+        o1(2)
+        o1(3)
+        c(2)
+        c(3)
         o2(0)
         o2(1)
         o2(2)

from contextlib import ExitStack

import concourse.masks as masks
import concourse.mybir as mybir

B, D_IN, UNITS = 1024, 512, 512
FLOPS = 4 * 2 * B * D_IN * UNITS

F32 = mybir.dt.float32
BF16 = mybir.dt.bfloat16
U32 = mybir.dt.uint32
U8 = mybir.dt.uint8
FP8 = mybir.dt.float8_e4m3fn
FP8X4 = mybir.dt.float8_e4m3fn_x4
ACT = mybir.ActivationFunctionType
ALU = mybir.AluOpType

P = 128
NA = 8


def tile_augru_pa_kernel(tc, input_x_bytes, input_x_scale, input_h, Wx_r, b_r, Wh_r, Wx_h, b_h, Wh_h, out):
    nc = tc.nc
    xb_v = input_x_bytes.rearrange("(p a) k -> p a k", a=NA)
    h_v = input_h.rearrange("(p a) k -> p a k", a=NA)
    out_v = out.rearrange("(p a) u -> p a u", a=NA)
    weights = {"xr": Wx_r, "hr": Wh_r, "hh": Wh_h, "xh": Wx_h}

    with ExitStack() as ctx:
        keep = ctx.enter_context(tc.tile_pool(name="keep", bufs=1))
        psum = ctx.enter_context(tc.psum_pool(name="psum", bufs=1))
        ctx.enter_context(tc.manual_schedule())

        ident = keep.tile([P, P], F32, name="ident", align_bytes=256)
        brows = keep.tile([P, P], BF16, name="brows")
        eye8 = keep.tile([P, 8], BF16, name="eye8")
        bias = keep.tile([P, 8], F32, name="bias")
        warm = keep.tile([P, 1], F32, name="warm")
        warm2 = keep.tile([P, 1], F32, name="warm2")
        xbytes = keep.tile([P, NA, D_IN], U8, name="xbytes", align_bytes=256)
        xscale = keep.tile([P, D_IN], F32, name="xscale", align_bytes=256)
        s4 = keep.tile([P, 4], F32, name="s4")
        xw = keep.tile([P, NA, D_IN], BF16, name="xw", align_bytes=256)
        hraw = keep.tile([P, NA, D_IN], BF16, name="hraw", align_bytes=256)
        wraw, wg, wc, wsc = {}, {}, {}, {}
        for w in weights:
            wraw[w] = keep.tile([P, 4, UNITS], BF16, name="wraw_" + w, align_bytes=256)
            wg[w] = keep.tile([P, 4 * UNITS], BF16, name="wg_" + w, align_bytes=256)
            wc[w] = keep.tile([P, UNITS], U32, name="wc_" + w, align_bytes=256)
            wsc[w] = keep.tile([P, UNITS], U8, name="wsc_" + w, align_bytes=256)
        ag, ac, asc = {}, {}, {}
        for s in ("x", "h"):
            for hf in (0, 1):
                ag[s, hf] = keep.tile([P, 2048], BF16, name="ag_%s%d" % (s, hf), align_bytes=256)
                ac[s, hf] = keep.tile([P, 512], U32, name="ac_%s%d" % (s, hf), align_bytes=256)
                asc[s, hf] = keep.tile([P, 512], U8, name="asc_%s%d" % (s, hf), align_bytes=256)
        r, t2, t3, o = {}, {}, {}, {}
        for i in range(8):
            r[i] = keep.tile([P, 512], F32, name="r_%d" % i, align_bytes=256)
            t2[i] = keep.tile([P, 512], F32, name="t2_%d" % i, align_bytes=256)
            t3[i] = keep.tile([P, 512], F32, name="t3_%d" % i, align_bytes=256)
            o[i] = keep.tile([P, 512], F32, name="o_%d" % i, align_bytes=256)
        banks = {}

        slots = {}
        for k, names in enumerate(
            (
                "Tsc a2 a6 b6 tt4",
                "Tx0 a3 a7 b7 tt5",
                "Tx1 Tx2 b2 c2 tt2 tt6",
                "Th0 Tx3 b3 c3 tt3 tt7",
                "Th1 b0 c0 tt0 c6",
                "bb b1 c1 tt1 c7",
                "a0 Th2 a4 b4 c4",
                "a1 Th3 a5 b5 c5",
            )
        ):
            for n in names.split(" "):
                slots[n] = k

        def bank(name):
            banks[name] = psum.tile([P, 512], F32, name=name, tag="bank%d" % slots[name])
            return banks[name]

        def ld_w(w, n0=0, n1=UNITS):
            nc.sync.dma_start(out=wraw[w][:, :, n0:n1], in_=weights[w].rearrange("(p j) n -> p j n", j=4)[:, :, n0:n1])

        def ld_x(a0, a1):
            nc.sync.dma_start(out=xbytes[:, a0:a1, :], in_=xb_v[:, a0:a1, :])

        def ld_h(a0, a1):
            nc.sync.dma_start(out=hraw[:, a0:a1, :], in_=h_v[:, a0:a1, :])

        def ld_sc():
            nc.sync.dma_start(out=s4[:], in_=input_x_scale.rearrange("o (p c) -> p (o c)", c=4))

        def spread_sc():
            bk = bank("Tsc")
            for c4 in range(4):
                nc.tensor.transpose(bk[:, P * c4 : P * c4 + P], s4[:, c4 : c4 + 1].to_broadcast([P, P]), ident[:])
            nc.scalar.copy(out=xscale[:].rearrange("p (i c) -> p i c", c=4), in_=bk[:].rearrange("p (c i) -> p i c", c=4))

        def il(w, eng, n0=0, n1=UNITS):
            dst = wg[w][:, 4 * n0 : 4 * n1].rearrange("p (c i j) -> p c j i", i=4, j=4)
            src = wraw[w][:, :, n0:n1].rearrange("p j (c i) -> p c j i", i=4)
            if eng == "V":
                nc.vector.tensor_copy(out=dst, in_=src)
            elif eng == "S":
                nc.scalar.copy(out=dst, in_=src)
            else:
                nc.gpsimd.tensor_scalar(out=dst, in0=src, scalar1=1.0, scalar2=0.0, op0=ALU.mult, op1=ALU.add)

        def qw(w):
            nc.vector.quantize_mx(out=wc[w][:].bitcast(FP8X4), scales=wsc[w][:], in_=wg[w][:])

        def widen(a):
            nc.vector.tensor_tensor(out=xw[:, a, :], in0=xbytes[:, a, :].bitcast(FP8), in1=xscale[:], op=ALU.mult)

        def turn(s, j):
            src = xw if s == "x" else hraw
            bv = bank("T%s%d" % (s, j))[:].rearrange("p (a u r) -> p a u r", a=2, u=2)
            for al in (0, 1):
                words = src[:, 2 * j + al, :].bitcast(F32)
                for u in (0, 1):
                    nc.tensor.transpose(bv[:, al, u, :], words[:, u:256:2], ident[:])

        def cp(s, j, eng="S"):
            hf, jl = divmod(j, 2)
            bv = banks["T%s%d" % (s, j)][:].rearrange("p (a u r) -> p a r u", a=2, u=2)
            dst = ag[s, hf][:, 1024 * jl : 1024 * jl + 1024].bitcast(F32).rearrange("p (a r u) -> p a r u", a=2, u=2)
            if eng == "S":
                nc.scalar.copy(out=dst, in_=bv)
            else:
                nc.vector.tensor_copy(out=dst, in_=bv)

        def qa(s, hf):
            nc.vector.quantize_mx(out=ac[s, hf][:].bitcast(FP8X4), scales=asc[s, hf][:], in_=ag[s, hf][:])

        def mx(dst, w, s, i, start, stop):
            hf, m = divmod(i, 4)
            cols = slice(P * m, P * m + P)
            nc.tensor.matmul_mx(
                out=dst[:],
                lhsT=wc[w][:, cols].bitcast(FP8X4),
                lhsT_scale=wsc[w][:, cols],
                rhs=ac[s, hf][:].bitcast(FP8X4),
                rhs_scale=asc[s, hf][:],
                start=start,
                stop=stop,
            )

        def a1(i):
            mx(bank("a%d" % i), "xr", "x", i, True, False)

        def a2(i):
            mx(banks["a%d" % i], "hr", "h", i, False, True)

        def sg(i):
            m = i % 4
            nc.scalar.activation(out=r[i][:], in_=banks["a%d" % i][:], func=ACT.Sigmoid, bias=bias[:, m : m + 1], scale=1.0)

        def b(i):
            mx(bank("b%d" % i), "hh", "h", i, True, True)

        def o1(i):
            nc.vector.tensor_tensor(out=t2[i][:], in0=r[i][:], in1=banks["b%d" % i][:], op=ALU.mult)

        def c(i):
            mx(bank("c%d" % i), "xh", "x", i, True, True)

        def o2(i):
            m = i % 4
            nc.vector.scalar_tensor_tensor(
                out=t3[i][:], in0=t2[i][:], scalar=bias[:, 4 + m : 5 + m], in1=banks["c%d" % i][:], op0=ALU.add, op1=ALU.add
            )

        def tt(i):
            bk = bank("tt%d" % i)
            for al in range(4):
                nc.tensor.transpose(bk[:, P * al : P * al + P], t3[i][:, P * al : P * al + P], ident[:])

        def th(i):
            nc.scalar.activation(out=o[i][:], in_=banks["tt%d" % i][:], func=ACT.Tanh)

        def st(i):
            hf, m = divmod(i, 4)
            nc.sync.dma_start(
                out=out_v[:, 4 * hf : 4 * hf + 4, P * m : P * m + P], in_=o[i][:].rearrange("p (a u) -> p a u", a=4)
            )

        def bb():
            nc.tensor.matmul(bank("bb")[:, 0:8], brows[:], eye8[:], start=True, stop=True)

        def bbcp():
            nc.scalar.copy(out=bias[:], in_=banks["bb"][:, 0:8])


        def keep_warm():
            bk = bank("warm")
            for q in range(2):
                nc.tensor.matmul(bk[:], wg["xr"][:, 0:P], wg["xr"][:, 0:512], start=True, stop=True)
        masks.make_identity(nc, ident[:])
        nc.vector.memset(warm[:], 0.0)
        nc.vector.memset(brows[:], 0.0)
        nc.vector.tensor_copy(out=eye8[:], in_=ident[:, 0:8])
        nc.scalar.activation(out=warm2[:], in_=warm[:], func=ACT.Sigmoid)

        ld_sc()
        ld_w("xr", 0, 256)
        ld_x(0, 2)
        ld_w("xr", 256, 512)
        ld_x(2, 4)
        ld_w("hr")
        nc.sync.dma_start(out=brows[0:4, :], in_=b_r.rearrange("(m p) -> m p", p=P))
        nc.sync.dma_start(out=brows[4:8, :], in_=b_h.rearrange("(m p) -> m p", p=P))
        ld_h(0, 4)
        ld_w("hh")
        ld_x(4, 8)
        ld_w("xh")
        ld_h(4, 8)

        spread_sc()
        il("xr", "V", 0, 256)
        widen(0)
        widen(1)
        il("xr", "S", 256, 512)
        turn("x", 0)
        widen(2)
        widen(3)
        turn("x", 1)
        il("hr", "S", 0, 256)
        il("hr", "V", 256, 512)
        cp("x", 0)
        cp("x", 1)
        il("hh", "S", 0, 128)
        turn("h", 0)
        turn("h", 1)
        qw("xr")
        qa("x", 0)
        for i in range(4):
            a1(i)
        bb()
        cp("h", 0)
        cp("h", 1)
        qw("hr")
        widen(4)
        qa("h", 0)
        for i in range(4):
            a2(i)
        il("hh", "S", 128, 512)
        bbcp()
        widen(5)
        widen(6)
        widen(7)
        qw("hh")
        turn("x",2)
        turn("x",3)
        b(0)
        b(1)
        il("xh", "V", 0, 256)
        il("xh", "S", 256, 512)
        qw("xh")
        sg(0)
        sg(1)
        turn("h",2)
        turn("h",3)
        o1(0)
        o1(1)
        cp("x",2)
        cp("x",3)
        cp("h",2)
        cp("h",3)
        c(0)
        c(1)
        b(2)
        b(3)
        qa("x",1)
        a1(4)
        a1(5)
        qa("h",1)
        sg(2)
        sg(3)
        a2(4)
        a2(5)
        a1(6)
        a2(6)
        a1(7)
        a2(7)
        o1(2)
        o1(3)
        c(2)
        c(3)
        o2(0)
        o2(1)
        o2(2)
        o2(3)
        sg(4)
        sg(5)
        sg(6)
        sg(7)
        b(4)
        b(5)
        b(6)
        b(7)
        o1(4)
        o1(5)
        o1(6)
        o1(7)
        tt(0)
        th(0)
        st(0)
        tt(1)
        th(1)
        st(1)
        tt(2)
        th(2)
        st(2)
        tt(3)
        th(3)
        st(3)
        c(4)
        c(5)
        c(6)
        c(7)
        o2(4)
        tt(4)
        th(4)
        st(4)
        o2(5)
        tt(5)
        th(5)
        st(5)
        o2(6)
        tt(6)
        th(6)
        st(6)
        o2(7)
        tt(7)
        th(7)
        st(7)
